import numpy as np
import ml_dtypes


def mxq(x, axis, fmt="e4m3"):
    dtype, down = {"e4m3": (ml_dtypes.float8_e4m3fn, 7), "e5m2": (ml_dtypes.float8_e5m2, 14)}[fmt]
    v = np.moveaxis(np.asarray(x, np.float32).astype(ml_dtypes.bfloat16).astype(np.float64), axis, -1)
    blocks = v.reshape(v.shape[:-1] + (-1, 32))
    amax = np.abs(blocks).max(-1, keepdims=True)
    byte = np.maximum(np.where(amax > 0, np.frexp(amax)[1] - 1 + 127, 0) - down, 1)
    scale = np.exp2(byte - 127.0)
    codes = (blocks / scale).astype(np.float32).astype(dtype).astype(np.float64)
    return np.moveaxis((codes * scale).reshape(v.shape), -1, axis)


WIDE = False


def mx_kscale(k):
    if not WIDE:
        return np.ones(k)
    levels = np.array([10, -10, 5, -5, 0])
    a = np.random.permutation(np.resize(levels, k // 512 * 4)).reshape(k // 512, 4)
    idx = np.arange(k)
    return np.exp2(a[idx // 512, idx % 128 // 32])


BF16 = ml_dtypes.bfloat16


def bf(x):
    return np.asarray(x, np.float32).astype(BF16)


def f64(x):
    return np.asarray(x).astype(np.float64)


E2M1 = np.array([0.0, 0.5, 1.0, 1.5, 2.0, 3.0, 4.0, 6.0, -0.0, -0.5, -1.0, -1.5, -2.0, -3.0, -4.0, -6.0])


def pack_weight(w, fmt):
    k, n = w.shape
    w = f64(bf(w)).reshape(k // 32, 32, n)
    amax = np.abs(w).max(1)
    if fmt == "e4m3":
        byte = np.frexp(amax)[1] - 1 + 127 - 7
    else:
        mant, ex = np.frexp(amax / 6.0)
        byte = np.where(mant > 0.5, ex, ex - 1) + 127
    byte = np.clip(np.where(amax > 0, byte, 1), 1, 254)
    scaled = (w * np.exp2(127.0 - byte)[:, None, :]).reshape(k, n).astype(np.float32)
    by_word = np.ascontiguousarray(scaled.reshape(k // 512, 128, 4, n).transpose(0, 1, 3, 2))
    if fmt == "e4m3":
        words = by_word.astype(ml_dtypes.float8_e4m3fn).view(np.uint8)
    else:
        c = by_word.astype(ml_dtypes.float4_e2m1fn).view(np.uint8) & 0xF
        words = c[..., 0::2] | (c[..., 1::2] << 4)
    return np.ascontiguousarray(words), np.ascontiguousarray(byte.astype(np.uint8).reshape(k // 512, 16, n))


def unpack_weight(words, scales, fmt):
    g, p, n, _ = words.shape
    if fmt == "e4m3":
        vals = np.ascontiguousarray(words).view(ml_dtypes.float8_e4m3fn).astype(np.float64)
    else:
        nib = np.empty((g, p, n, 4), np.uint8)
        nib[..., 0::2] = words & 0xF
        nib[..., 1::2] = words >> 4
        vals = E2M1[nib]
    vals = vals * np.repeat(np.exp2(scales.astype(np.float64) - 127.0), 8, axis=1)[..., None]
    return vals.transpose(0, 1, 3, 2).reshape(g * 512, n)


N, E, C = 16384, 256, 512
DENSITY = 0.01
FMT = "e4m3"


def setup_inputs():
    s, t = mx_kscale(N), mx_kscale(C)
    member = np.random.uniform(size=(N, E)) < DENSITY
    node_features = bf(np.random.standard_normal((N, C)) / s[:, None] * t[None, :])
    incidence = bf(member * s[:, None])
    words, scales = pack_weight(np.random.standard_normal((C, C)) * np.sqrt(E) / np.sqrt(DENSITY * N * C) / t[:, None], FMT)
    return {"node_features": node_features,
            "incidence": incidence,
            "W1_words": words,
            "W1_scales": scales,
            "b1": bf(np.random.standard_normal(C) * 0.1 * np.sqrt(E)),
            "edge_attention": bf(1.0 + np.random.standard_normal(E))}


def reference(node_features, incidence, W1_words, W1_scales, b1, edge_attention):
    agg = mxq(f64(incidence), 0, "e4m3").T @ mxq(f64(node_features), 0, "e4m3")
    lin = (mxq(agg, 1, "e4m3") @ unpack_weight(W1_words, W1_scales, FMT)) + f64(b1)
    a = f64(edge_attention)
    e = np.exp(a - a.max())
    attn = e / e.sum()
    return lin * attn[:, None]

@@ -1,0 +1,206 @@
+from contextlib import ExitStack
+
+import concourse.mybir as mybir
+
+BF16 = mybir.dt.bfloat16
+F32 = mybir.dt.float32
+I32 = mybir.dt.int32
+U32 = mybir.dt.uint32
+U8 = mybir.dt.uint8
+FP8X4 = mybir.dt.float8_e4m3fn_x4
+ALU = mybir.AluOpType
+ACT = mybir.ActivationFunctionType
+AXIS = mybir.AxisListType
+
+NODES, EDGES, CHANNELS = 16384, 256, 512
+FLOPS = 2 * NODES * EDGES * CHANNELS + 2 * EDGES * CHANNELS * CHANNELS
+
+P = 128
+PACK = 4
+K_PASS = P * PACK
+PASSES = NODES // K_PASS
+PLANE = CHANNELS // PACK
+HALVES = EDGES // P
+
+SCALAR_WORDS = 32
+VECTOR_WORDS = PLANE - SCALAR_WORDS
+
+PASSES_AHEAD = 6
+SIDE_WORK_PASS = 4
+ONE_COLUMN = 32
+
+
+def tile_heterogeneoustemporalhypergraphnn_pa_k_kernel(
+    tc, node_features, incidence, W1_words, W1_scales, b1, edge_attention, out
+):
+    nc = tc.nc
+    nf_dram = node_features.rearrange("(c p j) w -> c p (j w)", p=P, j=PACK)
+    inc_dram = incidence.rearrange("(c p j) e -> c p (j e)", p=P, j=PACK)
+
+    with ExitStack() as ctx:
+        const = ctx.enter_context(tc.tile_pool(name="const", bufs=1))
+        raw_pool = ctx.enter_context(tc.tile_pool(name="raw", bufs=PASSES_AHEAD + 1))
+        grouped_pool = ctx.enter_context(tc.tile_pool(name="grouped", bufs=3))
+        mx_pool = ctx.enter_context(tc.tile_pool(name="mx", bufs=3))
+        psum = ctx.enter_context(tc.psum_pool(name="psum", bufs=1))
+        ctx.enter_context(tc.manual_schedule())
+
+        nf_raw = {}
+        inc_raw = {}
+
+        def load_pass(c):
+            inc_raw[c] = raw_pool.tile([P, PACK, EDGES], BF16, name="inc_raw")
+            nc.sync.dma_start(out=inc_raw[c][:].rearrange("p j e -> p (j e)"), in_=inc_dram[c])
+            nf_raw[c] = raw_pool.tile([P, PACK, CHANNELS], BF16, name="nf_raw")
+            nc.sync.dma_start(out=nf_raw[c][:].rearrange("p j w -> p (j w)"), in_=nf_dram[c])
+
+        rows = const.tile([P, CHANNELS + EDGES], BF16)
+        ones = const.tile([P, P], BF16)
+        w1_scales = const.tile([P, CHANNELS], U8, align_bytes=64)
+        w1_words = const.tile([P, PACK * CHANNELS], U8, align_bytes=64)
+        nc.vector.memset(rows[:], 0.0)
+        nc.vector.memset(ones[:], 1.0)
+        nc.vector.memset(w1_scales[:].bitcast(I32), 0)
+        table_warmer = const.tile([P, 1], F32)
+        nc.scalar.activation(out=table_warmer[:], in_=ones[:, 0:1], func=ACT.Exp)
+        nc.scalar.dma_start(out=rows[0:1, 0:CHANNELS], in_=b1.rearrange("(o n) -> o n", o=1))
+        nc.scalar.dma_start(
+            out=rows[0:1, CHANNELS:], in_=edge_attention.rearrange("(o n) -> o n", o=1)
+        )
+
+        for c in range(PASSES_AHEAD):
+            load_pass(c)
+        nc.sync.dma_start(
+            out=w1_words[:].bitcast(I32),
+            in_=W1_words.rearrange("g p n t -> (g p) (n t)").bitcast(I32),
+        )
+        for quadrant in range(4):
+            nc.sync.dma_start(
+                out=w1_scales[32 * quadrant : 32 * quadrant + 4, :].bitcast(I32),
+                in_=W1_scales[0, 4 * quadrant : 4 * quadrant + 4, :].bitcast(I32),
+            )
+
+        agg_bank = [psum.tile([P, EDGES], F32, name="agg_bank%d" % t) for t in range(PACK)]
+        attn = const.tile([P, HALVES], F32)
+        bias_attn = const.tile([P, HALVES, CHANNELS], F32)
+
+        def softmax_and_bias():
+            bias_all = psum.tile([P, CHANNELS], F32)
+            logits = psum.tile([P, EDGES + HALVES * ONE_COLUMN], F32)
+            logits_all = logits[:, 0:EDGES]
+            logits_own = logits[:, EDGES:].rearrange("p (h r) -> p h r", r=ONE_COLUMN)
+            nc.tensor.matmul(out=logits_all, lhsT=ones[:], rhs=rows[:, CHANNELS:], start=True, stop=True)
+            for h in range(HALVES):
+                nc.tensor.matmul(
+                    out=logits_own[:, h, :],
+                    lhsT=rows[:, CHANNELS + P * h : CHANNELS + P * (h + 1)],
+                    rhs=ones[:, 0:ONE_COLUMN],
+                    start=True,
+                    stop=True,
+                )
+            nc.tensor.matmul(out=bias_all[:], lhsT=ones[:], rhs=rows[:, 0:CHANNELS], start=True, stop=True)
+            top = const.tile([P, 1], F32)
+            minus_top = const.tile([P, 1], F32)
+            nc.vector.tensor_reduce(out=top[:], in_=logits_all, axis=AXIS.X, op=ALU.max)
+            nc.vector.tensor_scalar_mul(out=minus_top[:], in0=top[:], scalar1=-1.0)
+            exp_all = const.tile([P, EDGES], F32)
+            exp_sum = const.tile([P, 1], F32)
+            exp_own = const.tile([P, HALVES], F32)
+            nc.scalar.activation(
+                out=exp_all[:], in_=logits_all, func=ACT.Exp, bias=minus_top[:], accum_out=exp_sum[:]
+            )
+            nc.scalar.activation(out=exp_own[:], in_=logits_own[:, :, 0], func=ACT.Exp, bias=minus_top[:])
+            one_over_sum = const.tile([P, 1], F32)
+            nc.vector.reciprocal(out=one_over_sum[:], in_=exp_sum[:])
+            nc.vector.tensor_scalar_mul(out=attn[:], in0=exp_own[:], scalar1=one_over_sum[:])
+            nc.scalar.activation(out=bias_attn[:, 0, :], in_=bias_all[:], func=ACT.Copy, scale=attn[:, 0:1])
+            nc.vector.tensor_scalar_mul(out=bias_attn[:, 1, :], in0=bias_all[:], scalar1=attn[:, 1:2])
+
+        for c in range(PASSES):
+            if c + PASSES_AHEAD < PASSES:
+                load_pass(c + PASSES_AHEAD)
+
+            inc_grouped = grouped_pool.tile([P, EDGES, PACK], BF16, align_bytes=64)
+            inc_words = mx_pool.tile([P, EDGES], U32, align_bytes=64)
+            inc_scales = mx_pool.tile([P, EDGES], U8, align_bytes=64)
+            nf_grouped = grouped_pool.tile([P, PACK, PLANE, PACK], BF16, align_bytes=64)
+            nf_words = mx_pool.tile([P, CHANNELS], U32, align_bytes=64)
+            nf_scales = mx_pool.tile([P, CHANNELS], U8, align_bytes=64)
+
+            nc.scalar.copy(
+                out=inc_grouped[:].rearrange("p (g i) j -> p g j i", i=4),
+                in_=inc_raw[c][:].rearrange("p j (g i) -> p g j i", i=4),
+            )
+            nc.scalar.copy(
+                out=nf_grouped[:, :, VECTOR_WORDS:, :].rearrange("p t q j -> p q j t"),
+                in_=nf_raw[c][:, :, PACK * VECTOR_WORDS :].rearrange("p j (q t) -> p q j t", t=PACK),
+            )
+            nc.vector.tensor_copy(
+                out=nf_grouped[:, :, 0:VECTOR_WORDS, :].rearrange("p t q j -> p q j t"),
+                in_=nf_raw[c][:, :, 0 : PACK * VECTOR_WORDS].rearrange("p j (q t) -> p q j t", t=PACK),
+            )
+            nc.vector.quantize_mx(
+                out=inc_words[:].bitcast(FP8X4),
+                scales=inc_scales[:],
+                in_=inc_grouped[:].rearrange("p e j -> p (e j)"),
+            )
+            nc.vector.quantize_mx(
+                out=nf_words[:].bitcast(FP8X4),
+                scales=nf_scales[:],
+                in_=nf_grouped[:].rearrange("p t q j -> p (t q j)"),
+            )
+            for t in range(PACK):
+                nc.tensor.matmul_mx(
+                    out=agg_bank[t][:],
+                    lhsT=nf_words[:, PLANE * t : PLANE * (t + 1)].bitcast(FP8X4),
+                    lhsT_scale=nf_scales[:, PLANE * t : PLANE * (t + 1)],
+                    rhs=inc_words[:].bitcast(FP8X4),
+                    rhs_scale=inc_scales[:],
+                    start=(c == 0),
+                    stop=(c == PASSES - 1),
+                )
+
+            if c == SIDE_WORK_PASS:
+                softmax_and_bias()
+
+        agg_planes = const.tile([P, PACK, EDGES], BF16)
+        for t in range(PACK):
+            if t % 2 == 0:
+                nc.vector.tensor_copy(out=agg_planes[:, t, :], in_=agg_bank[t][:])
+            else:
+                nc.scalar.copy(out=agg_planes[:, t, :], in_=agg_bank[t][:])
+        agg_grouped = const.tile([P, EDGES, PACK], BF16, align_bytes=64)
+        agg_words = const.tile([P, EDGES], U32, align_bytes=64)
+        agg_scales = const.tile([P, EDGES], U8, align_bytes=64)
+        half = [slice(P * h, P * (h + 1)) for h in range(HALVES)]
+        for h in range(HALVES):
+            nc.vector.tensor_copy(
+                out=agg_grouped[:, half[h], :], in_=agg_planes[:, :, half[h]].rearrange("p t e -> p e t")
+            )
+        for h in range(HALVES):
+            nc.vector.quantize_mx(
+                out=agg_words[:, half[h]].bitcast(FP8X4),
+                scales=agg_scales[:, half[h]],
+                in_=agg_grouped[:, half[h], :].rearrange("p e t -> p (e t)"),
+            )
+        for h in range(HALVES):
+            lin = psum.tile([P, CHANNELS], F32, name="lin%d" % h)
+            nc.tensor.matmul_mx(
+                out=lin[:],
+                lhsT=agg_words[:, half[h]].bitcast(FP8X4),
+                lhsT_scale=agg_scales[:, half[h]],
+                rhs=w1_words[:].bitcast(FP8X4),
+                rhs_scale=w1_scales[:],
+                start=True,
+                stop=True,
+            )
+            result = const.tile([P, CHANNELS], F32, name="result%d" % h)
+            nc.vector.scalar_tensor_tensor(
+                out=result[:],
+                in0=lin[:],
+                scalar=attn[:, h : h + 1],
+                in1=bias_attn[:, h, :],
+                op0=ALU.mult,
+                op1=ALU.add,
+            )
+            nc.sync.dma_start(out=out[half[h], :], in_=result[:])

@@ -1,6 +1,7 @@
 from contextlib import ExitStack
 
 import concourse.mybir as mybir
+from concourse.masks import make_identity
 
 BF16 = mybir.dt.bfloat16
 F32 = mybir.dt.float32
@@ -22,8 +23,8 @@ PASSES = NODES // K_PASS
 PLANE = CHANNELS // PACK
 HALVES = EDGES // P
 
-SCALAR_WORDS = 32
-VECTOR_WORDS = PLANE - SCALAR_WORDS
+SCALAR_COLUMNS = 128
+VECTOR_COLUMNS = CHANNELS - SCALAR_COLUMNS
 
 PASSES_AHEAD = 6
 SIDE_WORK_PASS = 4
@@ -58,6 +59,8 @@ def tile_heterogeneoustemporalhypergraphnn_pa_k_kernel(
         ones = const.tile([P, P], BF16)
         w1_scales = const.tile([P, CHANNELS], U8, align_bytes=64)
         w1_words = const.tile([P, PACK * CHANNELS], U8, align_bytes=64)
+        identity = const.tile([P, P], BF16)
+        make_identity(nc, identity[:])
         nc.vector.memset(rows[:], 0.0)
         nc.vector.memset(ones[:], 1.0)
         nc.vector.memset(w1_scales[:].bitcast(I32), 0)
@@ -80,7 +83,8 @@ def tile_heterogeneoustemporalhypergraphnn_pa_k_kernel(
                 in_=W1_scales[0, 4 * quadrant : 4 * quadrant + 4, :].bitcast(I32),
             )
 
-        agg_bank = [psum.tile([P, EDGES], F32, name="agg_bank%d" % t) for t in range(PACK)]
+        agg_bank = [psum.tile([P, CHANNELS], F32, name="agg_bank%d" % h) for h in range(HALVES)]
+        half = [slice(P * h, P * (h + 1)) for h in range(HALVES)]
         attn = const.tile([P, HALVES], F32)
         bias_attn = const.tile([P, HALVES, CHANNELS], F32)
 
@@ -123,7 +127,7 @@ def tile_heterogeneoustemporalhypergraphnn_pa_k_kernel(
             inc_grouped = grouped_pool.tile([P, EDGES, PACK], BF16, align_bytes=64)
             inc_words = mx_pool.tile([P, EDGES], U32, align_bytes=64)
             inc_scales = mx_pool.tile([P, EDGES], U8, align_bytes=64)
-            nf_grouped = grouped_pool.tile([P, PACK, PLANE, PACK], BF16, align_bytes=64)
+            nf_grouped = grouped_pool.tile([P, CHANNELS, PACK], BF16, align_bytes=64)
             nf_words = mx_pool.tile([P, CHANNELS], U32, align_bytes=64)
             nf_scales = mx_pool.tile([P, CHANNELS], U8, align_bytes=64)
 
@@ -132,12 +136,12 @@ def tile_heterogeneoustemporalhypergraphnn_pa_k_kernel(
                 in_=inc_raw[c][:].rearrange("p j (g i) -> p g j i", i=4),
             )
             nc.scalar.copy(
-                out=nf_grouped[:, :, VECTOR_WORDS:, :].rearrange("p t q j -> p q j t"),
-                in_=nf_raw[c][:, :, PACK * VECTOR_WORDS :].rearrange("p j (q t) -> p q j t", t=PACK),
+                out=nf_grouped[:, VECTOR_COLUMNS:, :].rearrange("p (g i) j -> p g j i", i=4),
+                in_=nf_raw[c][:, :, VECTOR_COLUMNS:].rearrange("p j (g i) -> p g j i", i=4),
             )
             nc.vector.tensor_copy(
-                out=nf_grouped[:, :, 0:VECTOR_WORDS, :].rearrange("p t q j -> p q j t"),
-                in_=nf_raw[c][:, :, 0 : PACK * VECTOR_WORDS].rearrange("p j (q t) -> p q j t", t=PACK),
+                out=nf_grouped[:, 0:VECTOR_COLUMNS, :].rearrange("p (g i) j -> p g j i", i=4),
+                in_=nf_raw[c][:, :, 0:VECTOR_COLUMNS].rearrange("p j (g i) -> p g j i", i=4),
             )
             nc.vector.quantize_mx(
                 out=inc_words[:].bitcast(FP8X4),
@@ -147,15 +151,15 @@ def tile_heterogeneoustemporalhypergraphnn_pa_k_kernel(
             nc.vector.quantize_mx(
                 out=nf_words[:].bitcast(FP8X4),
                 scales=nf_scales[:],
-                in_=nf_grouped[:].rearrange("p t q j -> p (t q j)"),
+                in_=nf_grouped[:].rearrange("p w j -> p (w j)"),
             )
-            for t in range(PACK):
+            for h in range(HALVES):
                 nc.tensor.matmul_mx(
-                    out=agg_bank[t][:],
-                    lhsT=nf_words[:, PLANE * t : PLANE * (t + 1)].bitcast(FP8X4),
-                    lhsT_scale=nf_scales[:, PLANE * t : PLANE * (t + 1)],
-                    rhs=inc_words[:].bitcast(FP8X4),
-                    rhs_scale=inc_scales[:],
+                    out=agg_bank[h][:],
+                    lhsT=inc_words[:, half[h]].bitcast(FP8X4),
+                    lhsT_scale=inc_scales[:, half[h]],
+                    rhs=nf_words[:].bitcast(FP8X4),
+                    rhs_scale=nf_scales[:],
                     start=(c == 0),
                     stop=(c == PASSES - 1),
                 )
@@ -163,20 +167,18 @@ def tile_heterogeneoustemporalhypergraphnn_pa_k_kernel(
             if c == SIDE_WORK_PASS:
                 softmax_and_bias()
 
-        agg_planes = const.tile([P, PACK, EDGES], BF16)
-        for t in range(PACK):
-            if t % 2 == 0:
-                nc.vector.tensor_copy(out=agg_planes[:, t, :], in_=agg_bank[t][:])
-            else:
-                nc.scalar.copy(out=agg_planes[:, t, :], in_=agg_bank[t][:])
+        agg_sorted = const.tile([P, HALVES, PACK, PLANE], BF16)
+        nc.vector.tensor_copy(out=agg_sorted[:, 0], in_=agg_bank[0][:].rearrange("p (q t) -> p t q", t=PACK))
+        nc.scalar.copy(out=agg_sorted[:, 1], in_=agg_bank[1][:].rearrange("p (q t) -> p t q", t=PACK))
+        agg_turned = [psum.tile([P, PACK, P], BF16, name="agg_turned%d" % h) for h in range(HALVES)]
+        for h in range(HALVES):
+            for t in range(PACK):
+                nc.tensor.transpose(agg_turned[h][:, t, :], agg_sorted[:, h, t, :], identity[:])
         agg_grouped = const.tile([P, EDGES, PACK], BF16, align_bytes=64)
         agg_words = const.tile([P, EDGES], U32, align_bytes=64)
         agg_scales = const.tile([P, EDGES], U8, align_bytes=64)
-        half = [slice(P * h, P * (h + 1)) for h in range(HALVES)]
-        for h in range(HALVES):
-            nc.vector.tensor_copy(
-                out=agg_grouped[:, half[h], :], in_=agg_planes[:, :, half[h]].rearrange("p t e -> p e t")
-            )
+        nc.vector.tensor_copy(out=agg_grouped[:, half[0], :], in_=agg_turned[0][:].rearrange("p t e -> p e t"))
+        nc.scalar.copy(out=agg_grouped[:, half[1], :], in_=agg_turned[1][:].rearrange("p t e -> p e t"))
         for h in range(HALVES):
             nc.vector.quantize_mx(
                 out=agg_words[:, half[h]].bitcast(FP8X4),

@@ -23,10 +23,10 @@ PASSES = NODES // K_PASS
 PLANE = CHANNELS // PACK
 HALVES = EDGES // P
 
-SCALAR_COLUMNS = 128
+SCALAR_COLUMNS = 144
 VECTOR_COLUMNS = CHANNELS - SCALAR_COLUMNS
 
-PASSES_AHEAD = 6
+PASSES_AHEAD = 8
 SIDE_WORK_PASS = 4
 ONE_COLUMN = 32
 
@@ -41,10 +41,9 @@ def tile_heterogeneoustemporalhypergraphnn_pa_k_kernel(
     with ExitStack() as ctx:
         const = ctx.enter_context(tc.tile_pool(name="const", bufs=1))
         raw_pool = ctx.enter_context(tc.tile_pool(name="raw", bufs=PASSES_AHEAD + 1))
-        grouped_pool = ctx.enter_context(tc.tile_pool(name="grouped", bufs=3))
-        mx_pool = ctx.enter_context(tc.tile_pool(name="mx", bufs=3))
+        grouped_pool = ctx.enter_context(tc.tile_pool(name="grouped", bufs=4))
+        mx_pool = ctx.enter_context(tc.tile_pool(name="mx", bufs=4))
         psum = ctx.enter_context(tc.psum_pool(name="psum", bufs=1))
-        ctx.enter_context(tc.manual_schedule())
 
         nf_raw = {}
         inc_raw = {}

@@ -20,14 +20,15 @@ P = 128
 PACK = 4
 K_PASS = P * PACK
 PASSES = NODES // K_PASS
+PAIRS = PASSES // 2
 PLANE = CHANNELS // PACK
 HALVES = EDGES // P
 
 SCALAR_COLUMNS = 144
 VECTOR_COLUMNS = CHANNELS - SCALAR_COLUMNS
 
-PASSES_AHEAD = 8
-SIDE_WORK_PASS = 4
+PAIRS_AHEAD = 4
+SIDE_WORK_PAIR = 2
 ONE_COLUMN = 32
 
 
@@ -40,19 +41,20 @@ def tile_heterogeneoustemporalhypergraphnn_pa_k_kernel(
 
     with ExitStack() as ctx:
         const = ctx.enter_context(tc.tile_pool(name="const", bufs=1))
-        raw_pool = ctx.enter_context(tc.tile_pool(name="raw", bufs=PASSES_AHEAD + 1))
-        grouped_pool = ctx.enter_context(tc.tile_pool(name="grouped", bufs=4))
-        mx_pool = ctx.enter_context(tc.tile_pool(name="mx", bufs=4))
+        raw_pool = ctx.enter_context(tc.tile_pool(name="raw", bufs=PAIRS_AHEAD + 1))
+        grouped_pool = ctx.enter_context(tc.tile_pool(name="grouped", bufs=3))
+        mx_pool = ctx.enter_context(tc.tile_pool(name="mx", bufs=3))
         psum = ctx.enter_context(tc.psum_pool(name="psum", bufs=1))
 
         nf_raw = {}
         inc_raw = {}
 
-        def load_pass(c):
-            inc_raw[c] = raw_pool.tile([P, PACK, EDGES], BF16, name="inc_raw")
-            nc.sync.dma_start(out=inc_raw[c][:].rearrange("p j e -> p (j e)"), in_=inc_dram[c])
-            nf_raw[c] = raw_pool.tile([P, PACK, CHANNELS], BF16, name="nf_raw")
-            nc.sync.dma_start(out=nf_raw[c][:].rearrange("p j w -> p (j w)"), in_=nf_dram[c])
+        def load_pair(d):
+            inc_raw[d] = raw_pool.tile([P, 2, PACK, EDGES], BF16, name="inc_raw")
+            nf_raw[d] = raw_pool.tile([P, 2, PACK, CHANNELS], BF16, name="nf_raw")
+            for s in range(2):
+                nc.sync.dma_start(out=inc_raw[d][:, s].rearrange("p j e -> p (j e)"), in_=inc_dram[2 * d + s])
+                nc.sync.dma_start(out=nf_raw[d][:, s].rearrange("p j w -> p (j w)"), in_=nf_dram[2 * d + s])
 
         rows = const.tile([P, CHANNELS + EDGES], BF16)
         ones = const.tile([P, P], BF16)
@@ -70,8 +72,8 @@ def tile_heterogeneoustemporalhypergraphnn_pa_k_kernel(
             out=rows[0:1, CHANNELS:], in_=edge_attention.rearrange("(o n) -> o n", o=1)
         )
 
-        for c in range(PASSES_AHEAD):
-            load_pass(c)
+        for d in range(PAIRS_AHEAD):
+            load_pair(d)
         nc.sync.dma_start(
             out=w1_words[:].bitcast(I32),
             in_=W1_words.rearrange("g p n t -> (g p) (n t)").bitcast(I32),
@@ -119,51 +121,53 @@ def tile_heterogeneoustemporalhypergraphnn_pa_k_kernel(
             nc.scalar.activation(out=bias_attn[:, 0, :], in_=bias_all[:], func=ACT.Copy, scale=attn[:, 0:1])
             nc.vector.tensor_scalar_mul(out=bias_attn[:, 1, :], in0=bias_all[:], scalar1=attn[:, 1:2])
 
-        for c in range(PASSES):
-            if c + PASSES_AHEAD < PASSES:
-                load_pass(c + PASSES_AHEAD)
+        for d in range(PAIRS):
+            if d + PAIRS_AHEAD < PAIRS:
+                load_pair(d + PAIRS_AHEAD)
 
-            inc_grouped = grouped_pool.tile([P, EDGES, PACK], BF16, align_bytes=64)
-            inc_words = mx_pool.tile([P, EDGES], U32, align_bytes=64)
-            inc_scales = mx_pool.tile([P, EDGES], U8, align_bytes=64)
-            nf_grouped = grouped_pool.tile([P, CHANNELS, PACK], BF16, align_bytes=64)
-            nf_words = mx_pool.tile([P, CHANNELS], U32, align_bytes=64)
-            nf_scales = mx_pool.tile([P, CHANNELS], U8, align_bytes=64)
+            inc_grouped = grouped_pool.tile([P, 2, EDGES, PACK], BF16, align_bytes=64)
+            inc_words = mx_pool.tile([P, 2, EDGES], U32, align_bytes=64)
+            inc_scales = mx_pool.tile([P, 2, EDGES], U8, align_bytes=64)
+            nf_grouped = grouped_pool.tile([P, 2, CHANNELS, PACK], BF16, align_bytes=64)
+            nf_words = mx_pool.tile([P, 2, CHANNELS], U32, align_bytes=64)
+            nf_scales = mx_pool.tile([P, 2, CHANNELS], U8, align_bytes=64)
 
-            nc.scalar.copy(
-                out=inc_grouped[:].rearrange("p (g i) j -> p g j i", i=4),
-                in_=inc_raw[c][:].rearrange("p j (g i) -> p g j i", i=4),
-            )
-            nc.scalar.copy(
-                out=nf_grouped[:, VECTOR_COLUMNS:, :].rearrange("p (g i) j -> p g j i", i=4),
-                in_=nf_raw[c][:, :, VECTOR_COLUMNS:].rearrange("p j (g i) -> p g j i", i=4),
-            )
-            nc.vector.tensor_copy(
-                out=nf_grouped[:, 0:VECTOR_COLUMNS, :].rearrange("p (g i) j -> p g j i", i=4),
-                in_=nf_raw[c][:, :, 0:VECTOR_COLUMNS].rearrange("p j (g i) -> p g j i", i=4),
-            )
-            nc.vector.quantize_mx(
-                out=inc_words[:].bitcast(FP8X4),
-                scales=inc_scales[:],
-                in_=inc_grouped[:].rearrange("p e j -> p (e j)"),
-            )
-            nc.vector.quantize_mx(
-                out=nf_words[:].bitcast(FP8X4),
-                scales=nf_scales[:],
-                in_=nf_grouped[:].rearrange("p w j -> p (w j)"),
-            )
-            for h in range(HALVES):
-                nc.tensor.matmul_mx(
-                    out=agg_bank[h][:],
-                    lhsT=inc_words[:, half[h]].bitcast(FP8X4),
-                    lhsT_scale=inc_scales[:, half[h]],
-                    rhs=nf_words[:].bitcast(FP8X4),
-                    rhs_scale=nf_scales[:],
-                    start=(c == 0),
-                    stop=(c == PASSES - 1),
+            for s in range(2):
+                nc.scalar.copy(
+                    out=inc_grouped[:, s].rearrange("p (g i) j -> p g j i", i=4),
+                    in_=inc_raw[d][:, s].rearrange("p j (g i) -> p g j i", i=4),
                 )
+                nc.scalar.copy(
+                    out=nf_grouped[:, s, VECTOR_COLUMNS:, :].rearrange("p (g i) j -> p g j i", i=4),
+                    in_=nf_raw[d][:, s, :, VECTOR_COLUMNS:].rearrange("p j (g i) -> p g j i", i=4),
+                )
+            nc.vector.tensor_copy(
+                out=nf_grouped[:, :, 0:VECTOR_COLUMNS, :].rearrange("p s (g i) j -> p s g j i", i=4),
+                in_=nf_raw[d][:, :, :, 0:VECTOR_COLUMNS].rearrange("p s j (g i) -> p s g j i", i=4),
+            )
+            nc.vector.quantize_mx(
+                out=inc_words[:].rearrange("p s e -> p (s e)").bitcast(FP8X4),
+                scales=inc_scales[:].rearrange("p s e -> p (s e)"),
+                in_=inc_grouped[:].rearrange("p s e j -> p (s e j)"),
+            )
+            nc.vector.quantize_mx(
+                out=nf_words[:].rearrange("p s w -> p (s w)").bitcast(FP8X4),
+                scales=nf_scales[:].rearrange("p s w -> p (s w)"),
+                in_=nf_grouped[:].rearrange("p s w j -> p (s w j)"),
+            )
+            for s in range(2):
+                for h in range(HALVES):
+                    nc.tensor.matmul_mx(
+                        out=agg_bank[h][:],
+                        lhsT=inc_words[:, s, half[h]].bitcast(FP8X4),
+                        lhsT_scale=inc_scales[:, s, half[h]],
+                        rhs=nf_words[:, s, :].bitcast(FP8X4),
+                        rhs_scale=nf_scales[:, s, :],
+                        start=(d == 0 and s == 0),
+                        stop=(d == PAIRS - 1 and s == 1),
+                    )
 
-            if c == SIDE_WORK_PASS:
+            if d == SIDE_WORK_PAIR:
                 softmax_and_bias()
 
         agg_sorted = const.tile([P, HALVES, PACK, PLANE], BF16)

@@ -46,6 +46,8 @@ def tile_heterogeneoustemporalhypergraphnn_pa_k_kernel(
         mx_pool = ctx.enter_context(tc.tile_pool(name="mx", bufs=3))
         psum = ctx.enter_context(tc.psum_pool(name="psum", bufs=1))
 
+        ctx.enter_context(tc.manual_schedule(engines={mybir.EngineType.SP}))
+
         nf_raw = {}
         inc_raw = {}
 
@@ -74,15 +76,17 @@ def tile_heterogeneoustemporalhypergraphnn_pa_k_kernel(
 
         for d in range(PAIRS_AHEAD):
             load_pair(d)
-        nc.sync.dma_start(
-            out=w1_words[:].bitcast(I32),
-            in_=W1_words.rearrange("g p n t -> (g p) (n t)").bitcast(I32),
-        )
-        for quadrant in range(4):
+
+        def load_w1():
             nc.sync.dma_start(
-                out=w1_scales[32 * quadrant : 32 * quadrant + 4, :].bitcast(I32),
-                in_=W1_scales[0, 4 * quadrant : 4 * quadrant + 4, :].bitcast(I32),
+                out=w1_words[:].bitcast(I32),
+                in_=W1_words.rearrange("g p n t -> (g p) (n t)").bitcast(I32),
             )
+            for quadrant in range(4):
+                nc.sync.dma_start(
+                    out=w1_scales[32 * quadrant : 32 * quadrant + 4, :].bitcast(I32),
+                    in_=W1_scales[0, 4 * quadrant : 4 * quadrant + 4, :].bitcast(I32),
+                )
 
         agg_bank = [psum.tile([P, CHANNELS], F32, name="agg_bank%d" % h) for h in range(HALVES)]
         half = [slice(P * h, P * (h + 1)) for h in range(HALVES)]
@@ -121,9 +125,17 @@ def tile_heterogeneoustemporalhypergraphnn_pa_k_kernel(
             nc.scalar.activation(out=bias_attn[:, 0, :], in_=bias_all[:], func=ACT.Copy, scale=attn[:, 0:1])
             nc.vector.tensor_scalar_mul(out=bias_attn[:, 1, :], in0=bias_all[:], scalar1=attn[:, 1:2])
 
+        def grouped_view(t):
+            return t.rearrange("p (g i) (u j) -> p g u i j", i=4, u=2)
+
+        def raw_view(t):
+            return t.rearrange("p (u j) (g i) -> p g u i j", i=4, u=2)
+
         for d in range(PAIRS):
             if d + PAIRS_AHEAD < PAIRS:
                 load_pair(d + PAIRS_AHEAD)
+            if d + PAIRS_AHEAD == PAIRS - 1:
+                load_w1()
 
             inc_grouped = grouped_pool.tile([P, 2, EDGES, PACK], BF16, align_bytes=64)
             inc_words = mx_pool.tile([P, 2, EDGES], U32, align_bytes=64)
@@ -133,18 +145,15 @@ def tile_heterogeneoustemporalhypergraphnn_pa_k_kernel(
             nf_scales = mx_pool.tile([P, 2, CHANNELS], U8, align_bytes=64)
 
             for s in range(2):
+                nc.scalar.copy(out=grouped_view(inc_grouped[:, s]), in_=raw_view(inc_raw[d][:, s]))
                 nc.scalar.copy(
-                    out=inc_grouped[:, s].rearrange("p (g i) j -> p g j i", i=4),
-                    in_=inc_raw[d][:, s].rearrange("p j (g i) -> p g j i", i=4),
+                    out=grouped_view(nf_grouped[:, s, VECTOR_COLUMNS:, :]),
+                    in_=raw_view(nf_raw[d][:, s, :, VECTOR_COLUMNS:]),
                 )
-                nc.scalar.copy(
-                    out=nf_grouped[:, s, VECTOR_COLUMNS:, :].rearrange("p (g i) j -> p g j i", i=4),
-                    in_=nf_raw[d][:, s, :, VECTOR_COLUMNS:].rearrange("p j (g i) -> p g j i", i=4),
+                nc.vector.tensor_copy(
+                    out=grouped_view(nf_grouped[:, s, 0:VECTOR_COLUMNS, :]),
+                    in_=raw_view(nf_raw[d][:, s, :, 0:VECTOR_COLUMNS]),
                 )
-            nc.vector.tensor_copy(
-                out=nf_grouped[:, :, 0:VECTOR_COLUMNS, :].rearrange("p s (g i) j -> p s g j i", i=4),
-                in_=nf_raw[d][:, :, :, 0:VECTOR_COLUMNS].rearrange("p s j (g i) -> p s g j i", i=4),
-            )
             nc.vector.quantize_mx(
                 out=inc_words[:].rearrange("p s e -> p (s e)").bitcast(FP8X4),
                 scales=inc_scales[:].rearrange("p s e -> p (s e)"),

@@ -28,7 +28,7 @@ SCALAR_COLUMNS = 144
 VECTOR_COLUMNS = CHANNELS - SCALAR_COLUMNS
 
 PAIRS_AHEAD = 4
-SIDE_WORK_PAIR = 2
+ROWS_PAIR = 11
 ONE_COLUMN = 32
 
 
@@ -69,13 +69,13 @@ def tile_heterogeneoustemporalhypergraphnn_pa_k_kernel(
         nc.vector.memset(w1_scales[:].bitcast(I32), 0)
         table_warmer = const.tile([P, 1], F32)
         nc.scalar.activation(out=table_warmer[:], in_=ones[:, 0:1], func=ACT.Exp)
-        nc.scalar.dma_start(out=rows[0:1, 0:CHANNELS], in_=b1.rearrange("(o n) -> o n", o=1))
-        nc.scalar.dma_start(
-            out=rows[0:1, CHANNELS:], in_=edge_attention.rearrange("(o n) -> o n", o=1)
-        )
 
         for d in range(PAIRS_AHEAD):
             load_pair(d)
+
+        def load_rows():
+            nc.sync.dma_start(out=rows[0:1, CHANNELS:], in_=edge_attention.rearrange("(o n) -> o n", o=1))
+            nc.sync.dma_start(out=rows[0:1, 0:CHANNELS], in_=b1.rearrange("(o n) -> o n", o=1))
 
         def load_w1():
             nc.sync.dma_start(
@@ -93,8 +93,12 @@ def tile_heterogeneoustemporalhypergraphnn_pa_k_kernel(
         attn = const.tile([P, HALVES], F32)
         bias_attn = const.tile([P, HALVES, CHANNELS], F32)
 
-        def softmax_and_bias():
-            bias_all = psum.tile([P, CHANNELS], F32)
+        bias_all = psum.tile([P, CHANNELS], F32)
+
+        def bias_product(h):
+            nc.scalar.activation(out=bias_attn[:, h, :], in_=bias_all[:], func=ACT.Copy, scale=attn[:, h : h + 1])
+
+        def softmax():
             logits = psum.tile([P, EDGES + HALVES * ONE_COLUMN], F32)
             logits_all = logits[:, 0:EDGES]
             logits_own = logits[:, EDGES:].rearrange("p (h r) -> p h r", r=ONE_COLUMN)
@@ -122,8 +126,6 @@ def tile_heterogeneoustemporalhypergraphnn_pa_k_kernel(
             one_over_sum = const.tile([P, 1], F32)
             nc.vector.reciprocal(out=one_over_sum[:], in_=exp_sum[:])
             nc.vector.tensor_scalar_mul(out=attn[:], in0=exp_own[:], scalar1=one_over_sum[:])
-            nc.scalar.activation(out=bias_attn[:, 0, :], in_=bias_all[:], func=ACT.Copy, scale=attn[:, 0:1])
-            nc.vector.tensor_scalar_mul(out=bias_attn[:, 1, :], in0=bias_all[:], scalar1=attn[:, 1:2])
 
         def grouped_view(t):
             return t.rearrange("p (g i) (u j) -> p g u i j", i=4, u=2)
@@ -136,6 +138,8 @@ def tile_heterogeneoustemporalhypergraphnn_pa_k_kernel(
                 load_pair(d + PAIRS_AHEAD)
             if d + PAIRS_AHEAD == PAIRS - 1:
                 load_w1()
+            if d + PAIRS_AHEAD == ROWS_PAIR:
+                load_rows()
 
             inc_grouped = grouped_pool.tile([P, 2, EDGES, PACK], BF16, align_bytes=64)
             inc_words = mx_pool.tile([P, 2, EDGES], U32, align_bytes=64)
@@ -154,16 +158,18 @@ def tile_heterogeneoustemporalhypergraphnn_pa_k_kernel(
                     out=grouped_view(nf_grouped[:, s, 0:VECTOR_COLUMNS, :]),
                     in_=raw_view(nf_raw[d][:, s, :, 0:VECTOR_COLUMNS]),
                 )
-            nc.vector.quantize_mx(
-                out=inc_words[:].rearrange("p s e -> p (s e)").bitcast(FP8X4),
-                scales=inc_scales[:].rearrange("p s e -> p (s e)"),
-                in_=inc_grouped[:].rearrange("p s e j -> p (s e j)"),
-            )
-            nc.vector.quantize_mx(
-                out=nf_words[:].rearrange("p s w -> p (s w)").bitcast(FP8X4),
-                scales=nf_scales[:].rearrange("p s w -> p (s w)"),
-                in_=nf_grouped[:].rearrange("p s w j -> p (s w j)"),
-            )
+            parts = [slice(0, 1), slice(1, 2)] if d in (0, PAIRS - 1) else [slice(0, 2)]
+            for part in parts:
+                nc.vector.quantize_mx(
+                    out=inc_words[:, part].rearrange("p s e -> p (s e)").bitcast(FP8X4),
+                    scales=inc_scales[:, part].rearrange("p s e -> p (s e)"),
+                    in_=inc_grouped[:, part].rearrange("p s e j -> p (s e j)"),
+                )
+                nc.vector.quantize_mx(
+                    out=nf_words[:, part].rearrange("p s w -> p (s w)").bitcast(FP8X4),
+                    scales=nf_scales[:, part].rearrange("p s w -> p (s w)"),
+                    in_=nf_grouped[:, part].rearrange("p s w j -> p (s w j)"),
+                )
             for s in range(2):
                 for h in range(HALVES):
                     nc.tensor.matmul_mx(
@@ -176,12 +182,18 @@ def tile_heterogeneoustemporalhypergraphnn_pa_k_kernel(
                         stop=(d == PAIRS - 1 and s == 1),
                     )
 
-            if d == SIDE_WORK_PAIR:
-                softmax_and_bias()
+            if d == PAIRS - 1:
+                softmax()
 
+        ctx.enter_context(
+            tc.manual_schedule(
+                engines={mybir.EngineType.SP, mybir.EngineType.DVE, mybir.EngineType.Activation}
+            )
+        )
         agg_sorted = const.tile([P, HALVES, PACK, PLANE], BF16)
         nc.vector.tensor_copy(out=agg_sorted[:, 0], in_=agg_bank[0][:].rearrange("p (q t) -> p t q", t=PACK))
         nc.scalar.copy(out=agg_sorted[:, 1], in_=agg_bank[1][:].rearrange("p (q t) -> p t q", t=PACK))
+        bias_product(0)
         agg_turned = [psum.tile([P, PACK, P], BF16, name="agg_turned%d" % h) for h in range(HALVES)]
         for h in range(HALVES):
             for t in range(PACK):
@@ -191,6 +203,7 @@ def tile_heterogeneoustemporalhypergraphnn_pa_k_kernel(
         agg_scales = const.tile([P, EDGES], U8, align_bytes=64)
         nc.vector.tensor_copy(out=agg_grouped[:, half[0], :], in_=agg_turned[0][:].rearrange("p t e -> p e t"))
         nc.scalar.copy(out=agg_grouped[:, half[1], :], in_=agg_turned[1][:].rearrange("p t e -> p e t"))
+        bias_product(1)
         for h in range(HALVES):
             nc.vector.quantize_mx(
                 out=agg_words[:, half[h]].bitcast(FP8X4),
@@ -208,13 +221,15 @@ def tile_heterogeneoustemporalhypergraphnn_pa_k_kernel(
                 start=True,
                 stop=True,
             )
-            result = const.tile([P, CHANNELS], F32, name="result%d" % h)
-            nc.vector.scalar_tensor_tensor(
-                out=result[:],
-                in0=lin[:],
-                scalar=attn[:, h : h + 1],
-                in1=bias_attn[:, h, :],
-                op0=ALU.mult,
-                op1=ALU.add,
-            )
-            nc.sync.dma_start(out=out[half[h], :], in_=result[:])
+            for v in range(2):
+                columns = slice(v * CHANNELS // 2, (v + 1) * CHANNELS // 2)
+                result = const.tile([P, CHANNELS // 2], F32, name="result%d%d" % (h, v))
+                nc.vector.scalar_tensor_tensor(
+                    out=result[:],
+                    in0=lin[:, columns],
+                    scalar=attn[:, h : h + 1],
+                    in1=bias_attn[:, h, columns],
+                    op0=ALU.mult,
+                    op1=ALU.add,
+                )
+                nc.sync.dma_start(out=out[half[h], columns], in_=result[:])

from contextlib import ExitStack

import concourse.mybir as mybir
from concourse.masks import make_identity

BF16 = mybir.dt.bfloat16
F32 = mybir.dt.float32
I32 = mybir.dt.int32
U32 = mybir.dt.uint32
U8 = mybir.dt.uint8
FP8X4 = mybir.dt.float8_e4m3fn_x4
ALU = mybir.AluOpType
ACT = mybir.ActivationFunctionType
AXIS = mybir.AxisListType

NODES, EDGES, CHANNELS = 16384, 256, 512
FLOPS = 2 * NODES * EDGES * CHANNELS + 2 * EDGES * CHANNELS * CHANNELS

P = 128
PACK = 4
K_PASS = P * PACK
PASSES = NODES // K_PASS
PAIRS = PASSES // 2
PLANE = CHANNELS // PACK
HALVES = EDGES // P

SCALAR_COLUMNS = 144
VECTOR_COLUMNS = CHANNELS - SCALAR_COLUMNS

PAIRS_AHEAD = 4
ROWS_PAIR = 11
ONE_COLUMN = 32


def tile_heterogeneoustemporalhypergraphnn_pa_k_kernel(
    tc, node_features, incidence, W1_words, W1_scales, b1, edge_attention, out
):
    nc = tc.nc
    nf_dram = node_features.rearrange("(c p j) w -> c p (j w)", p=P, j=PACK)
    inc_dram = incidence.rearrange("(c p j) e -> c p (j e)", p=P, j=PACK)

    with ExitStack() as ctx:
        const = ctx.enter_context(tc.tile_pool(name="const", bufs=1))
        raw_pool = ctx.enter_context(tc.tile_pool(name="raw", bufs=PAIRS_AHEAD + 1))
        grouped_pool = ctx.enter_context(tc.tile_pool(name="grouped", bufs=3))
        mx_pool = ctx.enter_context(tc.tile_pool(name="mx", bufs=3))
        psum = ctx.enter_context(tc.psum_pool(name="psum", bufs=1))

        ctx.enter_context(tc.manual_schedule(engines={mybir.EngineType.SP}))

        nf_raw = {}
        inc_raw = {}

        def load_pair(d):
            inc_raw[d] = raw_pool.tile([P, 2, PACK, EDGES], BF16, name="inc_raw")
            nf_raw[d] = raw_pool.tile([P, 2, PACK, CHANNELS], BF16, name="nf_raw")
            for s in range(2):
                nc.sync.dma_start(out=inc_raw[d][:, s].rearrange("p j e -> p (j e)"), in_=inc_dram[2 * d + s])
                nc.sync.dma_start(out=nf_raw[d][:, s].rearrange("p j w -> p (j w)"), in_=nf_dram[2 * d + s])

        rows = const.tile([P, CHANNELS + EDGES], BF16)
        ones = const.tile([P, P], BF16)
        w1_scales = const.tile([P, CHANNELS], U8, align_bytes=64)
        w1_words = const.tile([P, PACK * CHANNELS], U8, align_bytes=64)
        identity = const.tile([P, P], BF16)
        make_identity(nc, identity[:])
        nc.vector.memset(rows[:], 0.0)
        nc.vector.memset(ones[:], 1.0)
        nc.vector.memset(w1_scales[:].bitcast(I32), 0)
        table_warmer = const.tile([P, 1], F32)
        nc.scalar.activation(out=table_warmer[:], in_=ones[:, 0:1], func=ACT.Exp)

        for d in range(PAIRS_AHEAD):
            load_pair(d)

        def load_rows():
            nc.sync.dma_start(out=rows[0:1, CHANNELS:], in_=edge_attention.rearrange("(o n) -> o n", o=1))
            nc.sync.dma_start(out=rows[0:1, 0:CHANNELS], in_=b1.rearrange("(o n) -> o n", o=1))

        def load_w1():
            nc.sync.dma_start(
                out=w1_words[:].bitcast(I32),
                in_=W1_words.rearrange("g p n t -> (g p) (n t)").bitcast(I32),
            )
            for quadrant in range(4):
                nc.sync.dma_start(
                    out=w1_scales[32 * quadrant : 32 * quadrant + 4, :].bitcast(I32),
                    in_=W1_scales[0, 4 * quadrant : 4 * quadrant + 4, :].bitcast(I32),
                )

        agg_bank = [psum.tile([P, CHANNELS], F32, name="agg_bank%d" % h) for h in range(HALVES)]
        half = [slice(P * h, P * (h + 1)) for h in range(HALVES)]
        attn = const.tile([P, HALVES], F32)
        bias_attn = const.tile([P, HALVES, CHANNELS], F32)

        bias_all = psum.tile([P, CHANNELS], F32)

        def bias_product(h):
            nc.scalar.activation(out=bias_attn[:, h, :], in_=bias_all[:], func=ACT.Copy, scale=attn[:, h : h + 1])

        def softmax():
            logits = psum.tile([P, EDGES + HALVES * ONE_COLUMN], F32)
            logits_all = logits[:, 0:EDGES]
            logits_own = logits[:, EDGES:].rearrange("p (h r) -> p h r", r=ONE_COLUMN)
            nc.tensor.matmul(out=logits_all, lhsT=ones[:], rhs=rows[:, CHANNELS:], start=True, stop=True)
            for h in range(HALVES):
                nc.tensor.matmul(
                    out=logits_own[:, h, :],
                    lhsT=rows[:, CHANNELS + P * h : CHANNELS + P * (h + 1)],
                    rhs=ones[:, 0:ONE_COLUMN],
                    start=True,
                    stop=True,
                )
            nc.tensor.matmul(out=bias_all[:], lhsT=ones[:], rhs=rows[:, 0:CHANNELS], start=True, stop=True)
            top = const.tile([P, 1], F32)
            minus_top = const.tile([P, 1], F32)
            nc.vector.tensor_reduce(out=top[:], in_=logits_all, axis=AXIS.X, op=ALU.max)
            nc.vector.tensor_scalar_mul(out=minus_top[:], in0=top[:], scalar1=-1.0)
            exp_all = const.tile([P, EDGES], F32)
            exp_sum = const.tile([P, 1], F32)
            exp_own = const.tile([P, HALVES], F32)
            nc.scalar.activation(
                out=exp_all[:], in_=logits_all, func=ACT.Exp, bias=minus_top[:], accum_out=exp_sum[:]
            )
            nc.scalar.activation(out=exp_own[:], in_=logits_own[:, :, 0], func=ACT.Exp, bias=minus_top[:])
            one_over_sum = const.tile([P, 1], F32)
            nc.vector.reciprocal(out=one_over_sum[:], in_=exp_sum[:])
            nc.vector.tensor_scalar_mul(out=attn[:], in0=exp_own[:], scalar1=one_over_sum[:])

        def grouped_view(t):
            return t.rearrange("p (g i) (u j) -> p g u i j", i=4, u=2)

        def raw_view(t):
            return t.rearrange("p (u j) (g i) -> p g u i j", i=4, u=2)

        for d in range(PAIRS):
            if d + PAIRS_AHEAD < PAIRS:
                load_pair(d + PAIRS_AHEAD)
            if d + PAIRS_AHEAD == PAIRS - 1:
                load_w1()
            if d + PAIRS_AHEAD == ROWS_PAIR:
                load_rows()

            inc_grouped = grouped_pool.tile([P, 2, EDGES, PACK], BF16, align_bytes=64)
            inc_words = mx_pool.tile([P, 2, EDGES], U32, align_bytes=64)
            inc_scales = mx_pool.tile([P, 2, EDGES], U8, align_bytes=64)
            nf_grouped = grouped_pool.tile([P, 2, CHANNELS, PACK], BF16, align_bytes=64)
            nf_words = mx_pool.tile([P, 2, CHANNELS], U32, align_bytes=64)
            nf_scales = mx_pool.tile([P, 2, CHANNELS], U8, align_bytes=64)

            for s in range(2):
                nc.scalar.copy(out=grouped_view(inc_grouped[:, s]), in_=raw_view(inc_raw[d][:, s]))
                nc.scalar.copy(
                    out=grouped_view(nf_grouped[:, s, VECTOR_COLUMNS:, :]),
                    in_=raw_view(nf_raw[d][:, s, :, VECTOR_COLUMNS:]),
                )
                nc.vector.tensor_copy(
                    out=grouped_view(nf_grouped[:, s, 0:VECTOR_COLUMNS, :]),
                    in_=raw_view(nf_raw[d][:, s, :, 0:VECTOR_COLUMNS]),
                )
            parts = [slice(0, 1), slice(1, 2)] if d in (0, PAIRS - 1) else [slice(0, 2)]
            for part in parts:
                nc.vector.quantize_mx(
                    out=inc_words[:, part].rearrange("p s e -> p (s e)").bitcast(FP8X4),
                    scales=inc_scales[:, part].rearrange("p s e -> p (s e)"),
                    in_=inc_grouped[:, part].rearrange("p s e j -> p (s e j)"),
                )
                nc.vector.quantize_mx(
                    out=nf_words[:, part].rearrange("p s w -> p (s w)").bitcast(FP8X4),
                    scales=nf_scales[:, part].rearrange("p s w -> p (s w)"),
                    in_=nf_grouped[:, part].rearrange("p s w j -> p (s w j)"),
                )
            for s in range(2):
                for h in range(HALVES):
                    nc.tensor.matmul_mx(
                        out=agg_bank[h][:],
                        lhsT=inc_words[:, s, half[h]].bitcast(FP8X4),
                        lhsT_scale=inc_scales[:, s, half[h]],
                        rhs=nf_words[:, s, :].bitcast(FP8X4),
                        rhs_scale=nf_scales[:, s, :],
                        start=(d == 0 and s == 0),
                        stop=(d == PAIRS - 1 and s == 1),
                    )

            if d == PAIRS - 1:
                softmax()

        ctx.enter_context(
            tc.manual_schedule(
                engines={mybir.EngineType.SP, mybir.EngineType.DVE, mybir.EngineType.Activation}
            )
        )
        agg_sorted = const.tile([P, HALVES, PACK, PLANE], BF16)
        nc.vector.tensor_copy(out=agg_sorted[:, 0], in_=agg_bank[0][:].rearrange("p (q t) -> p t q", t=PACK))
        nc.scalar.copy(out=agg_sorted[:, 1], in_=agg_bank[1][:].rearrange("p (q t) -> p t q", t=PACK))
        bias_product(0)
        agg_turned = [psum.tile([P, PACK, P], BF16, name="agg_turned%d" % h) for h in range(HALVES)]
        for h in range(HALVES):
            for t in range(PACK):
                nc.tensor.transpose(agg_turned[h][:, t, :], agg_sorted[:, h, t, :], identity[:])
        agg_grouped = const.tile([P, EDGES, PACK], BF16, align_bytes=64)
        agg_words = const.tile([P, EDGES], U32, align_bytes=64)
        agg_scales = const.tile([P, EDGES], U8, align_bytes=64)
        nc.vector.tensor_copy(out=agg_grouped[:, half[0], :], in_=agg_turned[0][:].rearrange("p t e -> p e t"))
        nc.scalar.copy(out=agg_grouped[:, half[1], :], in_=agg_turned[1][:].rearrange("p t e -> p e t"))
        bias_product(1)
        for h in range(HALVES):
            nc.vector.quantize_mx(
                out=agg_words[:, half[h]].bitcast(FP8X4),
                scales=agg_scales[:, half[h]],
                in_=agg_grouped[:, half[h], :].rearrange("p e t -> p (e t)"),
            )
        for h in range(HALVES):
            lin = psum.tile([P, CHANNELS], F32, name="lin%d" % h)
            nc.tensor.matmul_mx(
                out=lin[:],
                lhsT=agg_words[:, half[h]].bitcast(FP8X4),
                lhsT_scale=agg_scales[:, half[h]],
                rhs=w1_words[:].bitcast(FP8X4),
                rhs_scale=w1_scales[:],
                start=True,
                stop=True,
            )
            for v in range(2):
                columns = slice(v * CHANNELS // 2, (v + 1) * CHANNELS // 2)
                result = const.tile([P, CHANNELS // 2], F32, name="result%d%d" % (h, v))
                nc.vector.scalar_tensor_tensor(
                    out=result[:],
                    in0=lin[:, columns],
                    scalar=attn[:, h : h + 1],
                    in1=bias_attn[:, h, columns],
                    op0=ALU.mult,
                    op1=ALU.add,
                )
                nc.sync.dma_start(out=out[half[h], columns], in_=result[:])
